import numpy as np
import ml_dtypes


def mxq(x, axis, fmt="e4m3"):
    dtype, down = {"e4m3": (ml_dtypes.float8_e4m3fn, 7), "e5m2": (ml_dtypes.float8_e5m2, 14)}[fmt]
    v = np.moveaxis(np.asarray(x, np.float32).astype(ml_dtypes.bfloat16).astype(np.float64), axis, -1)
    blocks = v.reshape(v.shape[:-1] + (-1, 32))
    amax = np.abs(blocks).max(-1, keepdims=True)
    byte = np.maximum(np.where(amax > 0, np.frexp(amax)[1] - 1 + 127, 0) - down, 1)
    scale = np.exp2(byte - 127.0)
    codes = (blocks / scale).astype(np.float32).astype(dtype).astype(np.float64)
    return np.moveaxis((codes * scale).reshape(v.shape), -1, axis)


WIDE = False


def mx_kscale(k):
    if not WIDE:
        return np.ones(k)
    levels = np.array([10, -10, 5, -5, 0])
    a = np.random.permutation(np.resize(levels, k // 512 * 4)).reshape(k // 512, 4)
    idx = np.arange(k)
    return np.exp2(a[idx // 512, idx % 128 // 32])


BF16 = ml_dtypes.bfloat16


def bf(x):
    return np.asarray(x, np.float32).astype(BF16)


def f64(x):
    return np.asarray(x).astype(np.float64)


NA, NB, ND, ED = 32, 32, 1024, 1024
K1 = 2 * ED


def setup_inputs():
    s, t = mx_kscale(K1), mx_kscale(ED)
    return {"edge_embeds": bf(np.random.standard_normal((NA, NB, K1)) * s),
            "a_proj": bf(np.random.standard_normal((NA, ED)) * 0.5 * t),
            "b_proj": bf(np.random.standard_normal((NB, ED)) * 0.5 * t),
            "We": bf(np.random.standard_normal((K1, ED)) * 0.7 / np.sqrt(K1) / s[:, None] * t),
            "be1": bf(np.random.standard_normal(ED) * 0.3 * t),
            "We2": bf(np.random.standard_normal((ED, ED)) * 0.5 / np.sqrt(ED) / t[:, None]),
            "be2": bf(np.random.standard_normal(ED) * 0.1)}


def reference(edge_embeds, a_proj, b_proj, We, be1, We2, be2):
    h = f64(a_proj)[:, None, :] + f64(b_proj)[None, :, :] + (mxq(f64(edge_embeds), 2, "e4m3") @ mxq(f64(We), 0, "e4m3")) + f64(be1)
    h = np.maximum(h, 0.0)
    edge_latent = np.maximum((mxq(h, 2, "e4m3") @ mxq(f64(We2), 0, "e4m3")) + f64(be2), 0.0)
    sum_a = edge_latent.sum(axis=1)
    sum_b = edge_latent.sum(axis=0)
    return edge_latent, sum_a, sum_b

@@ -1,0 +1,332 @@
+from contextlib import ExitStack
+
+import concourse.masks as masks
+import concourse.mybir as mybir
+
+F32 = mybir.dt.float32
+BF16 = mybir.dt.bfloat16
+U32 = mybir.dt.uint32
+U8 = mybir.dt.uint8
+FP8X4 = mybir.dt.float8_e4m3fn_x4
+ADD = mybir.AluOpType.add
+RELU = mybir.ActivationFunctionType.Relu
+AXIS_X = mybir.AxisListType.X
+
+P = 128
+PACK = 4
+K_PASS = P * PACK
+BANK = 512
+
+NA, NB = 32, 32
+ROWS = NA * NB
+K1 = 2048
+ED = 1024
+ROW_TILES = ROWS // P
+A_PER_TILE = P // NB
+PASSES_1 = K1 // K_PASS
+PASSES_2 = ED // K_PASS
+OUT_HALVES = ED // BANK
+OUT_TILES = ED // P
+SUM_COLS = A_PER_TILE + NB
+
+FLOPS = 2 * ROWS * K1 * ED + 2 * ROWS * ED * ED
+
+
+def tile_bipartiteneuralmessagepassinglayer_pa_kernel(
+    tc, edge_embeds, a_proj, b_proj, We, be1, We2, be2, out_0, out_1, out_2
+):
+    nc = tc.nc
+    x_rows = edge_embeds.rearrange("a b k -> (a b) k")
+    latent_rows = out_0.rearrange("a b f -> (a b) f")
+
+    with ExitStack() as ctx:
+        keep = ctx.enter_context(tc.tile_pool(name="keep", bufs=1))
+        grouped_w = ctx.enter_context(tc.tile_pool(name="grouped_w", bufs=2))
+        grouped_x = ctx.enter_context(tc.tile_pool(name="grouped_x", bufs=2))
+        terms_pool = ctx.enter_context(tc.tile_pool(name="terms", bufs=3))
+        hidden = ctx.enter_context(tc.tile_pool(name="hidden", bufs=5))
+        latent_pool = ctx.enter_context(tc.tile_pool(name="latent", bufs=3))
+        psum_x = ctx.enter_context(tc.psum_pool(name="psum_x", bufs=2))
+        psum_plain = ctx.enter_context(tc.psum_pool(name="psum_plain", bufs=1))
+        psum_h = ctx.enter_context(tc.psum_pool(name="psum_h", bufs=2))
+        psum_o = ctx.enter_context(tc.psum_pool(name="psum_o", bufs=2))
+        psum_s = ctx.enter_context(tc.psum_pool(name="psum_s", bufs=1))
+        ctx.enter_context(tc.manual_schedule())
+
+        node_rows = keep.tile([P, ED], BF16)
+        nc.vector.memset(node_rows[:], 0.0)
+        nc.scalar.dma_start(out=node_rows[0:NA, :], in_=a_proj)
+        nc.scalar.dma_start(out=node_rows[NA : NA + NB, :], in_=b_proj)
+        nc.scalar.dma_start(
+            out=node_rows[NA + NB : NA + NB + 1, :], in_=be1.rearrange("(o e) -> o e", o=1)
+        )
+        be2_row = keep.tile([P, ED], BF16)
+        nc.vector.memset(be2_row[:], 0.0)
+        nc.scalar.dma_start(out=be2_row[0:1, :], in_=be2.rearrange("(o f) -> o f", o=1))
+
+        we_raw = keep.tile([P, PASSES_1, PACK, ED], BF16)
+        for c in range(PASSES_1):
+            nc.sync.dma_start(
+                out=we_raw[:, c].rearrange("p (u e) n -> p u (e n)", u=2),
+                in_=We[c * K_PASS : (c + 1) * K_PASS, :].rearrange(
+                    "(u p e) n -> p u (e n)", u=2, e=2
+                ),
+            )
+        x_raw = keep.tile([P, ROW_TILES * K1], BF16)
+        we2_raw = keep.tile([P, PASSES_2, PACK, ED], BF16)
+
+        def load_x(rt):
+            nc.sync.dma_start(
+                out=x_raw[:, rt * K1 : (rt + 1) * K1], in_=x_rows[rt * P : (rt + 1) * P, :]
+            )
+
+        for rt in range(3):
+            load_x(rt)
+        for g in range(PASSES_2):
+            nc.sync.dma_start(
+                out=we2_raw[:, g],
+                in_=We2[g * K_PASS : (g + 1) * K_PASS, :].rearrange("(t p) n -> p t n", p=P),
+            )
+        for rt in range(3, ROW_TILES):
+            load_x(rt)
+
+        ident = keep.tile([P, P], F32)
+        masks.make_identity(nc, ident[:])
+        ones = keep.tile([P, P], BF16)
+        nc.vector.memset(ones[:], 1.0)
+        table_warmer = keep.tile([P, 1], F32)
+        nc.scalar.activation(out=table_warmer[:], in_=ident[:, 0:1], func=RELU)
+
+        pick = keep.tile([P, NA, NB], BF16)
+        nc.vector.tensor_tensor(
+            out=pick[:],
+            in0=ident[:, 0:NA].unsqueeze(2).to_broadcast([P, NA, NB]),
+            in1=ident[:, NA : NA + NB].unsqueeze(1).to_broadcast([P, NA, NB]),
+            op=ADD,
+        )
+        nc.vector.tensor_scalar_add(
+            out=pick[:], in0=pick[:], scalar1=ident[:, NA + NB : NA + NB + 1]
+        )
+        pick_cols = pick[:].rearrange("k i j -> k (i j)")
+
+        summer = keep.tile([P, SUM_COLS], F32)
+        nc.vector.tensor_reduce(
+            out=summer[:, 0:A_PER_TILE],
+            in_=ident[:].rearrange("r (a j) -> r a j", a=A_PER_TILE),
+            axis=AXIS_X,
+            op=ADD,
+        )
+        nc.vector.tensor_reduce(
+            out=summer[:, A_PER_TILE:SUM_COLS],
+            in_=ident[:].rearrange("r (a j) -> r j a", a=A_PER_TILE),
+            axis=AXIS_X,
+            op=ADD,
+        )
+
+        be2_all = keep.tile([P, ED], F32)
+        for half in range(OUT_HALVES):
+            cols = slice(half * BANK, (half + 1) * BANK)
+            be2_ps = psum_plain.tile([P, BANK], F32, tag="plain")
+            nc.tensor.matmul(be2_ps[:], lhsT=ones[:], rhs=be2_row[:, cols], start=True, stop=True)
+            nc.scalar.copy(out=be2_all[:, cols], in_=be2_ps[:])
+
+        sums_t = keep.tile([P, OUT_TILES * (NA + NB)], F32)
+        nc.vector.memset(sums_t[:], 0.0)
+        sums_view = sums_t[:].rearrange("f (t c) -> f t c", c=NA + NB)
+
+        we_codes = keep.tile([P, PASSES_1 * ED], U32, align_bytes=64)
+        we_scales = keep.tile([P, PASSES_1 * ED], U8, align_bytes=64)
+        we2_codes = keep.tile([P, PASSES_2 * ED], U32, align_bytes=64)
+        we2_scales = keep.tile([P, PASSES_2 * ED], U8, align_bytes=64)
+        x_codes = keep.tile([P, ROW_TILES * PASSES_1 * P], U32, align_bytes=64)
+        x_scales = keep.tile([P, ROW_TILES * PASSES_1 * P], U8, align_bytes=64)
+
+        def regroup_weights(raw):
+            grouped = grouped_w.tile([P, ED * PACK], BF16, align_bytes=64)
+            by_column = grouped[:].rearrange("p (n t) -> p n t", t=PACK)
+            first, second = slice(0, ED // 2), slice(ED // 2, ED)
+            nc.vector.tensor_copy(
+                out=by_column[:, first, :].rearrange("p (n i) t -> p n t i", i=4),
+                in_=raw[:, :, first].rearrange("p t (n i) -> p n t i", i=4),
+            )
+            nc.scalar.copy(
+                out=by_column[:, second, :].rearrange("p (n i) t -> p n t i", i=4),
+                in_=raw[:, :, second].rearrange("p t (n i) -> p n t i", i=4),
+            )
+            return grouped
+
+        def quantise_weights(grouped, codes, scales, which_pass):
+            cols = slice(which_pass * ED, (which_pass + 1) * ED)
+            nc.vector.quantize_mx(
+                out=codes[:, cols].bitcast(FP8X4), scales=scales[:, cols], in_=grouped[:]
+            )
+
+        x_words = x_raw[:].bitcast(F32)
+        words_per_row = K1 // 2
+
+        def transpose_x(rt):
+            grouped = grouped_x.tile([P, PASSES_1 * P * PACK], BF16, align_bytes=64)
+            grouped_words = grouped[:].bitcast(F32).rearrange(
+                "p (c r u) -> p c r u", c=PASSES_1, u=2
+            )
+            for pair in range(PASSES_1 // 2):
+                xt = psum_x.tile([P, 4, P], F32)
+                for block in range(4):
+                    first = rt * words_per_row + (pair * 4 + block) * P
+                    nc.tensor.transpose(xt[:, block, :], x_words[:, first : first + P], ident[:])
+                nc.scalar.copy(
+                    out=grouped_words[:, 2 * pair : 2 * pair + 2, :, :],
+                    in_=xt[:].rearrange("p (c u) r -> p c r u", u=2),
+                )
+            return grouped
+
+        def quantise_x(rt, grouped):
+            cols = slice(rt * PASSES_1 * P, (rt + 1) * PASSES_1 * P)
+            nc.vector.quantize_mx(
+                out=x_codes[:, cols].bitcast(FP8X4), scales=x_scales[:, cols], in_=grouped[:]
+            )
+
+        def node_terms(rt, g, terms):
+            terms_ps = psum_plain.tile([P, PACK, P], F32, tag="plain")
+            for t in range(PACK):
+                e_tile = g * PACK + t
+                nc.tensor.matmul(
+                    terms_ps[:, t, :],
+                    lhsT=node_rows[:, e_tile * P : (e_tile + 1) * P],
+                    rhs=pick_cols[:, rt * P : (rt + 1) * P],
+                    start=True,
+                    stop=True,
+                )
+            nc.scalar.copy(
+                out=terms[:, g * BANK : (g + 1) * BANK].rearrange("p (r t) -> p r t", t=PACK),
+                in_=terms_ps[:].rearrange("p t r -> p r t"),
+            )
+
+        def first_product(rt, g, terms, h_grouped):
+            h_ps = psum_h.tile([P, PACK, P], F32)
+            for t in range(PACK):
+                e_tile = g * PACK + t
+                for c in range(PASSES_1):
+                    w_cols = slice(c * ED + e_tile * P, c * ED + (e_tile + 1) * P)
+                    r_cols = slice((rt * PASSES_1 + c) * P, (rt * PASSES_1 + c + 1) * P)
+                    nc.tensor.matmul_mx(
+                        out=h_ps[:, t, :],
+                        lhsT=we_codes[:, w_cols].bitcast(FP8X4),
+                        lhsT_scale=we_scales[:, w_cols],
+                        rhs=x_codes[:, r_cols].bitcast(FP8X4),
+                        rhs_scale=x_scales[:, r_cols],
+                        start=(c == 0),
+                        stop=(c == PASSES_1 - 1),
+                    )
+            part = slice(g * BANK, (g + 1) * BANK)
+            nc.vector.tensor_tensor(
+                out=h_grouped[:, part].rearrange("p (r t) -> p r t", t=PACK),
+                in0=h_ps[:].rearrange("p t r -> p r t"),
+                in1=terms[:, part].rearrange("p (r t) -> p r t", t=PACK),
+                op=ADD,
+            )
+
+        def quantise_hidden(h_grouped):
+            nc.vector.tensor_scalar_max(out=h_grouped[:], in0=h_grouped[:], scalar1=0.0)
+            h_codes = hidden.tile([P, PASSES_2 * P], U32, align_bytes=64)
+            h_scales = hidden.tile([P, PASSES_2 * P], U8, align_bytes=64)
+            nc.vector.quantize_mx(
+                out=h_codes[:].bitcast(FP8X4), scales=h_scales[:], in_=h_grouped[:]
+            )
+            return h_codes, h_scales
+
+        def second_product(rt, h_codes, h_scales):
+            latent = latent_pool.tile([P, ED], F32)
+            for half in range(OUT_HALVES):
+                o_ps = psum_o.tile([P, BANK], F32)
+                for g in range(PASSES_2):
+                    r_cols = slice(g * P, (g + 1) * P)
+                    f_cols = slice(g * ED + half * BANK, g * ED + (half + 1) * BANK)
+                    nc.tensor.matmul_mx(
+                        out=o_ps[:],
+                        lhsT=h_codes[:, r_cols].bitcast(FP8X4),
+                        lhsT_scale=h_scales[:, r_cols],
+                        rhs=we2_codes[:, f_cols].bitcast(FP8X4),
+                        rhs_scale=we2_scales[:, f_cols],
+                        start=(g == 0),
+                        stop=(g == PASSES_2 - 1),
+                    )
+                cols = slice(half * BANK, (half + 1) * BANK)
+                nc.vector.tensor_tensor(
+                    out=latent[:, cols], in0=o_ps[:], in1=be2_all[:, cols], op=ADD
+                )
+                nc.scalar.activation(out=latent[:, cols], in_=latent[:, cols], func=RELU)
+            nc.sync.dma_start(out=latent_rows[rt * P : (rt + 1) * P, :], in_=latent[:])
+            return latent
+
+        def add_to_sums(rt, latent):
+            s_ps = psum_s.tile([P, OUT_TILES, SUM_COLS], F32)
+            for f_tile in range(OUT_TILES):
+                nc.tensor.matmul(
+                    s_ps[:, f_tile, :],
+                    lhsT=latent[:, f_tile * P : (f_tile + 1) * P],
+                    rhs=summer[:],
+                    start=True,
+                    stop=True,
+                )
+            first_a = rt * A_PER_TILE
+            nc.vector.tensor_copy(
+                out=sums_view[:, :, first_a : first_a + A_PER_TILE], in_=s_ps[:, :, 0:A_PER_TILE]
+            )
+            nc.vector.tensor_tensor(
+                out=sums_view[:, :, NA : NA + NB],
+                in0=s_ps[:, :, A_PER_TILE:SUM_COLS],
+                in1=sums_view[:, :, NA : NA + NB],
+                op=ADD,
+            )
+
+        grouped_of = {}
+        for c in range(PASSES_1):
+            grouped_of[c] = regroup_weights(we_raw[:, c])
+            if c > 0:
+                quantise_weights(grouped_of[c - 1], we_codes, we_scales, c - 1)
+        quantise_weights(grouped_of[PASSES_1 - 1], we_codes, we_scales, PASSES_1 - 1)
+
+        AHEAD, BEHIND_2, BEHIND_S = 1, 3, 4
+        we2_grouped_of, terms_of, h_of, latent_of = {}, {}, {}, {}
+        for step in range(-AHEAD, ROW_TILES + BEHIND_S):
+            ahead = step + AHEAD
+            prepares = ahead < ROW_TILES
+            multiplies = 0 <= step < ROW_TILES
+            if prepares:
+                x_grouped = transpose_x(ahead)
+                quantise_x(ahead, x_grouped)
+                terms = terms_pool.tile([P, PASSES_2 * P * PACK], F32)
+                terms_of[ahead] = terms
+            if multiplies:
+                h_grouped = hidden.tile([P, PASSES_2 * P * PACK], BF16, align_bytes=64)
+            for g in range(PASSES_2):
+                if multiplies:
+                    first_product(step, g, terms_of[step], h_grouped)
+                if prepares:
+                    node_terms(ahead, g, terms_of[ahead])
+            if multiplies:
+                h_of[step] = quantise_hidden(h_grouped)
+            if 1 <= step <= PASSES_2:
+                quantise_weights(we2_grouped_of[step - 1], we2_codes, we2_scales, step - 1)
+            if 0 <= step < PASSES_2:
+                we2_grouped_of[step] = regroup_weights(we2_raw[:, step])
+            if 0 <= step - BEHIND_2 < ROW_TILES:
+                rt = step - BEHIND_2
+                latent_of[rt] = second_product(rt, h_of[rt][0], h_of[rt][1])
+            if 0 <= step - BEHIND_S < ROW_TILES:
+                rt = step - BEHIND_S
+                add_to_sums(rt, latent_of[rt])
+
+        pairs = OUT_TILES // 2
+        back_ps = psum_plain.tile([P, pairs, P], F32, tag="plain")
+        for q in range(pairs):
+            nc.tensor.transpose(back_ps[:, q, :], sums_t[:, q * P : (q + 1) * P], ident[:])
+        back = keep.tile([P, pairs, P], F32)
+        nc.vector.tensor_copy(out=back[:], in_=back_ps[:])
+        sum_a_view = out_1.rearrange("i (q v f) -> v i q f", q=pairs, v=2)
+        sum_b_view = out_2.rearrange("j (q v f) -> v j q f", q=pairs, v=2)
+        for v in range(2):
+            first = v * (NA + NB)
+            nc.sync.dma_start(out=sum_a_view[v], in_=back[first : first + NA, :, :])
+            nc.sync.dma_start(out=sum_b_view[v], in_=back[first + NA : first + NA + NB, :, :])

@@ -44,56 +44,56 @@ def tile_bipartiteneuralmessagepassinglayer_pa_kernel(
         grouped_w = ctx.enter_context(tc.tile_pool(name="grouped_w", bufs=2))
         grouped_x = ctx.enter_context(tc.tile_pool(name="grouped_x", bufs=2))
         terms_pool = ctx.enter_context(tc.tile_pool(name="terms", bufs=3))
-        hidden = ctx.enter_context(tc.tile_pool(name="hidden", bufs=5))
-        latent_pool = ctx.enter_context(tc.tile_pool(name="latent", bufs=3))
+        hidden = ctx.enter_context(tc.tile_pool(name="hidden", bufs=3))
+        latent_pool = ctx.enter_context(tc.tile_pool(name="latent", bufs=4))
         psum_x = ctx.enter_context(tc.psum_pool(name="psum_x", bufs=2))
-        psum_plain = ctx.enter_context(tc.psum_pool(name="psum_plain", bufs=1))
-        psum_h = ctx.enter_context(tc.psum_pool(name="psum_h", bufs=2))
-        psum_o = ctx.enter_context(tc.psum_pool(name="psum_o", bufs=2))
-        psum_s = ctx.enter_context(tc.psum_pool(name="psum_s", bufs=1))
+        psum_plain = ctx.enter_context(tc.psum_pool(name="psum_plain", bufs=2))
+        psum_mx = ctx.enter_context(tc.psum_pool(name="psum_mx", bufs=4))
         ctx.enter_context(tc.manual_schedule())
 
         node_rows = keep.tile([P, ED], BF16)
-        nc.vector.memset(node_rows[:], 0.0)
-        nc.scalar.dma_start(out=node_rows[0:NA, :], in_=a_proj)
-        nc.scalar.dma_start(out=node_rows[NA : NA + NB, :], in_=b_proj)
-        nc.scalar.dma_start(
-            out=node_rows[NA + NB : NA + NB + 1, :], in_=be1.rearrange("(o e) -> o e", o=1)
-        )
-        be2_row = keep.tile([P, ED], BF16)
-        nc.vector.memset(be2_row[:], 0.0)
-        nc.scalar.dma_start(out=be2_row[0:1, :], in_=be2.rearrange("(o f) -> o f", o=1))
+        nc.sync.dma_start(out=node_rows[0:NA, :], in_=a_proj)
+        nc.sync.dma_start(out=node_rows[NA : NA + NB, :], in_=b_proj)
+        nc.sync.dma_start(out=node_rows[NA + NB : P, :], in_=be1.partition_broadcast(P - NA - NB))
 
-        we_raw = keep.tile([P, PASSES_1, PACK, ED], BF16)
-        for c in range(PASSES_1):
-            nc.sync.dma_start(
-                out=we_raw[:, c].rearrange("p (u e) n -> p u (e n)", u=2),
-                in_=We[c * K_PASS : (c + 1) * K_PASS, :].rearrange(
-                    "(u p e) n -> p u (e n)", u=2, e=2
-                ),
-            )
-        x_raw = keep.tile([P, ROW_TILES * K1], BF16)
+        we_raw = keep.tile([P, OUT_HALVES, PASSES_1, PACK, BANK], BF16)
         we2_raw = keep.tile([P, PASSES_2, PACK, ED], BF16)
+        x_raw = keep.tile([P, ROW_TILES * K1], BF16)
+        be2_all = keep.tile([P, ED], BF16)
+
+        def load_we_piece(half, c):
+            for u in range(2):
+                first = c * K_PASS + u * (K_PASS // 2)
+                nc.sync.dma_start(
+                    out=we_raw[:, half, c, 2 * u : 2 * u + 2, :],
+                    in_=We[
+                        first : first + K_PASS // 2, half * BANK : (half + 1) * BANK
+                    ].rearrange("(p e) n -> p e n", e=2),
+                )
 
         def load_x(rt):
             nc.sync.dma_start(
                 out=x_raw[:, rt * K1 : (rt + 1) * K1], in_=x_rows[rt * P : (rt + 1) * P, :]
             )
 
-        for rt in range(3):
-            load_x(rt)
+        for c in range(PASSES_1):
+            load_we_piece(0, c)
+        load_x(0)
+        load_x(1)
+        for c in range(PASSES_1):
+            load_we_piece(1, c)
+            load_x(2 + c)
+        load_x(6)
+        load_x(7)
         for g in range(PASSES_2):
             nc.sync.dma_start(
                 out=we2_raw[:, g],
                 in_=We2[g * K_PASS : (g + 1) * K_PASS, :].rearrange("(t p) n -> p t n", p=P),
             )
-        for rt in range(3, ROW_TILES):
-            load_x(rt)
+        nc.sync.dma_start(out=be2_all[:], in_=be2.partition_broadcast(P))
 
         ident = keep.tile([P, P], F32)
         masks.make_identity(nc, ident[:])
-        ones = keep.tile([P, P], BF16)
-        nc.vector.memset(ones[:], 1.0)
         table_warmer = keep.tile([P, 1], F32)
         nc.scalar.activation(out=table_warmer[:], in_=ident[:, 0:1], func=RELU)
 
@@ -123,13 +123,6 @@ def tile_bipartiteneuralmessagepassinglayer_pa_kernel(
             op=ADD,
         )
 
-        be2_all = keep.tile([P, ED], F32)
-        for half in range(OUT_HALVES):
-            cols = slice(half * BANK, (half + 1) * BANK)
-            be2_ps = psum_plain.tile([P, BANK], F32, tag="plain")
-            nc.tensor.matmul(be2_ps[:], lhsT=ones[:], rhs=be2_row[:, cols], start=True, stop=True)
-            nc.scalar.copy(out=be2_all[:, cols], in_=be2_ps[:])
-
         sums_t = keep.tile([P, OUT_TILES * (NA + NB)], F32)
         nc.vector.memset(sums_t[:], 0.0)
         sums_view = sums_t[:].rearrange("f (t c) -> f t c", c=NA + NB)
@@ -140,11 +133,25 @@ def tile_bipartiteneuralmessagepassinglayer_pa_kernel(
         we2_scales = keep.tile([P, PASSES_2 * ED], U8, align_bytes=64)
         x_codes = keep.tile([P, ROW_TILES * PASSES_1 * P], U32, align_bytes=64)
         x_scales = keep.tile([P, ROW_TILES * PASSES_1 * P], U8, align_bytes=64)
+        h_codes = keep.tile([P, ROW_TILES * PASSES_2 * P], U32, align_bytes=64)
+        h_scales = keep.tile([P, ROW_TILES * PASSES_2 * P], U8, align_bytes=64)
 
-        def regroup_weights(raw):
-            grouped = grouped_w.tile([P, ED * PACK], BF16, align_bytes=64)
+        pieces = []
+        for half in range(OUT_HALVES):
+            for c in range(PASSES_1):
+                pieces.append((we_raw[:, half, c], we_codes, we_scales, c * ED + half * BANK))
+        for g in range(PASSES_2):
+            for half in range(OUT_HALVES):
+                cols = slice(half * BANK, (half + 1) * BANK)
+                pieces.append((we2_raw[:, g, :, cols], we2_codes, we2_scales, g * ED + half * BANK))
+        grouped_of = {}
+
+        def regroup_piece(index):
+            raw = pieces[index][0]
+            grouped = grouped_w.tile([P, BANK * PACK], BF16, align_bytes=64)
+            grouped_of[index] = grouped
             by_column = grouped[:].rearrange("p (n t) -> p n t", t=PACK)
-            first, second = slice(0, ED // 2), slice(ED // 2, ED)
+            first, second = slice(0, BANK // 2), slice(BANK // 2, BANK)
             nc.vector.tensor_copy(
                 out=by_column[:, first, :].rearrange("p (n i) t -> p n t i", i=4),
                 in_=raw[:, :, first].rearrange("p t (n i) -> p n t i", i=4),
@@ -153,12 +160,14 @@ def tile_bipartiteneuralmessagepassinglayer_pa_kernel(
                 out=by_column[:, second, :].rearrange("p (n i) t -> p n t i", i=4),
                 in_=raw[:, :, second].rearrange("p t (n i) -> p n t i", i=4),
             )
-            return grouped
 
-        def quantise_weights(grouped, codes, scales, which_pass):
-            cols = slice(which_pass * ED, (which_pass + 1) * ED)
+        def quantise_piece(index):
+            codes, scales, first_col = pieces[index][1:]
+            cols = slice(first_col, first_col + BANK)
             nc.vector.quantize_mx(
-                out=codes[:, cols].bitcast(FP8X4), scales=scales[:, cols], in_=grouped[:]
+                out=codes[:, cols].bitcast(FP8X4),
+                scales=scales[:, cols],
+                in_=grouped_of[index][:],
             )
 
         x_words = x_raw[:].bitcast(F32)
@@ -171,9 +180,9 @@ def tile_bipartiteneuralmessagepassinglayer_pa_kernel(
             )
             for pair in range(PASSES_1 // 2):
                 xt = psum_x.tile([P, 4, P], F32)
-                for block in range(4):
-                    first = rt * words_per_row + (pair * 4 + block) * P
-                    nc.tensor.transpose(xt[:, block, :], x_words[:, first : first + P], ident[:])
+                for quarter in range(4):
+                    first = rt * words_per_row + (pair * 4 + quarter) * P
+                    nc.tensor.transpose(xt[:, quarter, :], x_words[:, first : first + P], ident[:])
                 nc.scalar.copy(
                     out=grouped_words[:, 2 * pair : 2 * pair + 2, :, :],
                     in_=xt[:].rearrange("p (c u) r -> p c r u", u=2),
@@ -186,7 +195,7 @@ def tile_bipartiteneuralmessagepassinglayer_pa_kernel(
                 out=x_codes[:, cols].bitcast(FP8X4), scales=x_scales[:, cols], in_=grouped[:]
             )
 
-        def node_terms(rt, g, terms):
+        def node_terms(rt, g):
             terms_ps = psum_plain.tile([P, PACK, P], F32, tag="plain")
             for t in range(PACK):
                 e_tile = g * PACK + t
@@ -197,13 +206,12 @@ def tile_bipartiteneuralmessagepassinglayer_pa_kernel(
                     start=True,
                     stop=True,
                 )
-            nc.scalar.copy(
-                out=terms[:, g * BANK : (g + 1) * BANK].rearrange("p (r t) -> p r t", t=PACK),
-                in_=terms_ps[:].rearrange("p t r -> p r t"),
-            )
+            terms = terms_pool.tile([P, P, PACK], F32)
+            nc.scalar.copy(out=terms[:], in_=terms_ps[:].rearrange("p t r -> p r t"))
+            return terms
 
-        def first_product(rt, g, terms, h_grouped):
-            h_ps = psum_h.tile([P, PACK, P], F32)
+        def first_product(rt, g, terms):
+            h_ps = psum_mx.tile([P, PACK, P], F32, tag="mx")
             for t in range(PACK):
                 e_tile = g * PACK + t
                 for c in range(PASSES_1):
@@ -218,29 +226,29 @@ def tile_bipartiteneuralmessagepassinglayer_pa_kernel(
                         start=(c == 0),
                         stop=(c == PASSES_1 - 1),
                     )
-            part = slice(g * BANK, (g + 1) * BANK)
+            h_grouped = hidden.tile([P, P, PACK], BF16, align_bytes=64)
             nc.vector.tensor_tensor(
-                out=h_grouped[:, part].rearrange("p (r t) -> p r t", t=PACK),
-                in0=h_ps[:].rearrange("p t r -> p r t"),
-                in1=terms[:, part].rearrange("p (r t) -> p r t", t=PACK),
-                op=ADD,
+                out=h_grouped[:], in0=h_ps[:].rearrange("p t r -> p r t"), in1=terms[:], op=ADD
             )
+            return h_grouped
 
-        def quantise_hidden(h_grouped):
+        def relu_hidden(h_grouped):
             nc.vector.tensor_scalar_max(out=h_grouped[:], in0=h_grouped[:], scalar1=0.0)
-            h_codes = hidden.tile([P, PASSES_2 * P], U32, align_bytes=64)
-            h_scales = hidden.tile([P, PASSES_2 * P], U8, align_bytes=64)
-            nc.vector.quantize_mx(
-                out=h_codes[:].bitcast(FP8X4), scales=h_scales[:], in_=h_grouped[:]
-            )
-            return h_codes, h_scales
 
-        def second_product(rt, h_codes, h_scales):
+        def quantise_hidden(rt, g, h_grouped):
+            cols = slice((rt * PASSES_2 + g) * P, (rt * PASSES_2 + g + 1) * P)
+            nc.vector.quantize_mx(
+                out=h_codes[:, cols].bitcast(FP8X4),
+                scales=h_scales[:, cols],
+                in_=h_grouped[:].rearrange("p r t -> p (r t)"),
+            )
+
+        def second_product(rt):
             latent = latent_pool.tile([P, ED], F32)
             for half in range(OUT_HALVES):
-                o_ps = psum_o.tile([P, BANK], F32)
+                o_ps = psum_mx.tile([P, BANK], F32, tag="mx")
                 for g in range(PASSES_2):
-                    r_cols = slice(g * P, (g + 1) * P)
+                    r_cols = slice((rt * PASSES_2 + g) * P, (rt * PASSES_2 + g + 1) * P)
                     f_cols = slice(g * ED + half * BANK, g * ED + (half + 1) * BANK)
                     nc.tensor.matmul_mx(
                         out=o_ps[:],
@@ -260,7 +268,7 @@ def tile_bipartiteneuralmessagepassinglayer_pa_kernel(
             return latent
 
         def add_to_sums(rt, latent):
-            s_ps = psum_s.tile([P, OUT_TILES, SUM_COLS], F32)
+            s_ps = psum_plain.tile([P, OUT_TILES, SUM_COLS], F32, tag="plain")
             for f_tile in range(OUT_TILES):
                 nc.tensor.matmul(
                     s_ps[:, f_tile, :],
@@ -280,43 +288,45 @@ def tile_bipartiteneuralmessagepassinglayer_pa_kernel(
                 op=ADD,
             )
 
-        grouped_of = {}
-        for c in range(PASSES_1):
-            grouped_of[c] = regroup_weights(we_raw[:, c])
-            if c > 0:
-                quantise_weights(grouped_of[c - 1], we_codes, we_scales, c - 1)
-        quantise_weights(grouped_of[PASSES_1 - 1], we_codes, we_scales, PASSES_1 - 1)
+        for index in range(PASSES_1):
+            regroup_piece(index)
+            if index > 0:
+                quantise_piece(index - 1)
+        quantise_piece(PASSES_1 - 1)
 
-        AHEAD, BEHIND_2, BEHIND_S = 1, 3, 4
-        we2_grouped_of, terms_of, h_of, latent_of = {}, {}, {}, {}
-        for step in range(-AHEAD, ROW_TILES + BEHIND_S):
-            ahead = step + AHEAD
-            prepares = ahead < ROW_TILES
-            multiplies = 0 <= step < ROW_TILES
-            if prepares:
-                x_grouped = transpose_x(ahead)
-                quantise_x(ahead, x_grouped)
-                terms = terms_pool.tile([P, PASSES_2 * P * PACK], F32)
-                terms_of[ahead] = terms
-            if multiplies:
-                h_grouped = hidden.tile([P, PASSES_2 * P * PACK], BF16, align_bytes=64)
-            for g in range(PASSES_2):
-                if multiplies:
-                    first_product(step, g, terms_of[step], h_grouped)
-                if prepares:
-                    node_terms(ahead, g, terms_of[ahead])
-            if multiplies:
-                h_of[step] = quantise_hidden(h_grouped)
-            if 1 <= step <= PASSES_2:
-                quantise_weights(we2_grouped_of[step - 1], we2_codes, we2_scales, step - 1)
-            if 0 <= step < PASSES_2:
-                we2_grouped_of[step] = regroup_weights(we2_raw[:, step])
-            if 0 <= step - BEHIND_2 < ROW_TILES:
-                rt = step - BEHIND_2
-                latent_of[rt] = second_product(rt, h_of[rt][0], h_of[rt][1])
-            if 0 <= step - BEHIND_S < ROW_TILES:
-                rt = step - BEHIND_S
-                add_to_sums(rt, latent_of[rt])
+        units = PASSES_2 * ROW_TILES
+        terms_of, h_of = {}, {}
+        for unit in range(-1, units + 1):
+            following, before = unit + 1, unit - 1
+            if following < units:
+                next_g, next_rt = divmod(following, ROW_TILES)
+                if next_g == 0:
+                    x_grouped = transpose_x(next_rt)
+                    quantise_x(next_rt, x_grouped)
+            if 0 <= unit < units:
+                g, rt = divmod(unit, ROW_TILES)
+                h_of[unit] = first_product(rt, g, terms_of[unit])
+            if following < units:
+                terms_of[following] = node_terms(next_rt, next_g)
+            if before >= 0:
+                relu_hidden(h_of[before])
+            if 0 <= unit < units:
+                index = PASSES_1 + unit // 2
+                if unit % 2 == 0:
+                    regroup_piece(index)
+                else:
+                    quantise_piece(index)
+            if before >= 0:
+                g, rt = divmod(before, ROW_TILES)
+                quantise_hidden(rt, g, h_of[before])
+
+        SUMS_BEHIND = 2
+        latent_of = {}
+        for rt in range(ROW_TILES + SUMS_BEHIND):
+            if rt < ROW_TILES:
+                latent_of[rt] = second_product(rt)
+            if rt >= SUMS_BEHIND:
+                add_to_sums(rt - SUMS_BEHIND, latent_of[rt - SUMS_BEHIND])
 
         pairs = OUT_TILES // 2
         back_ps = psum_plain.tile([P, pairs, P], F32, tag="plain")

@@ -27,7 +27,6 @@ PASSES_1 = K1 // K_PASS
 PASSES_2 = ED // K_PASS
 OUT_HALVES = ED // BANK
 OUT_TILES = ED // P
-SUM_COLS = A_PER_TILE + NB
 
 FLOPS = 2 * ROWS * K1 * ED + 2 * ROWS * ED * ED
 
@@ -109,23 +108,31 @@ def tile_bipartiteneuralmessagepassinglayer_pa_kernel(
         )
         pick_cols = pick[:].rearrange("k i j -> k (i j)")
 
-        summer = keep.tile([P, SUM_COLS], F32)
+        of_a_node = keep.tile([P, A_PER_TILE], F32)
         nc.vector.tensor_reduce(
-            out=summer[:, 0:A_PER_TILE],
+            out=of_a_node[:],
             in_=ident[:].rearrange("r (a j) -> r a j", a=A_PER_TILE),
             axis=AXIS_X,
             op=ADD,
         )
+        of_b_node = keep.tile([P, NB], F32)
         nc.vector.tensor_reduce(
-            out=summer[:, A_PER_TILE:SUM_COLS],
+            out=of_b_node[:],
             in_=ident[:].rearrange("r (a j) -> r j a", a=A_PER_TILE),
             axis=AXIS_X,
             op=ADD,
         )
-
-        sums_t = keep.tile([P, OUT_TILES * (NA + NB)], F32)
-        nc.vector.memset(sums_t[:], 0.0)
-        sums_view = sums_t[:].rearrange("f (t c) -> f t c", c=NA + NB)
+        summers = keep.tile([P, ROW_TILES, P], F32)
+        nc.vector.memset(summers[:], 0.0)
+        for rt in range(ROW_TILES):
+            first_a = rt * A_PER_TILE
+            nc.vector.tensor_copy(
+                out=summers[:, rt, first_a : first_a + A_PER_TILE], in_=of_a_node[:]
+            )
+        nc.vector.tensor_copy(
+            out=summers[:, :, NA : NA + NB],
+            in_=of_b_node[:].unsqueeze(1).to_broadcast([P, ROW_TILES, NB]),
+        )
 
         we_codes = keep.tile([P, PASSES_1 * ED], U32, align_bytes=64)
         we_scales = keep.tile([P, PASSES_1 * ED], U8, align_bytes=64)
@@ -267,26 +274,15 @@ def tile_bipartiteneuralmessagepassinglayer_pa_kernel(
             nc.sync.dma_start(out=latent_rows[rt * P : (rt + 1) * P, :], in_=latent[:])
             return latent
 
-        def add_to_sums(rt, latent):
-            s_ps = psum_plain.tile([P, OUT_TILES, SUM_COLS], F32, tag="plain")
-            for f_tile in range(OUT_TILES):
+        def add_to_sums(rt, latent, sums_ps):
+            for half in range(OUT_HALVES):
                 nc.tensor.matmul(
-                    s_ps[:, f_tile, :],
-                    lhsT=latent[:, f_tile * P : (f_tile + 1) * P],
-                    rhs=summer[:],
-                    start=True,
-                    stop=True,
+                    sums_ps[half][:],
+                    lhsT=summers[:, rt, :],
+                    rhs=latent[:, half * BANK : (half + 1) * BANK],
+                    start=(rt == 0),
+                    stop=(rt == ROW_TILES - 1),
                 )
-            first_a = rt * A_PER_TILE
-            nc.vector.tensor_copy(
-                out=sums_view[:, :, first_a : first_a + A_PER_TILE], in_=s_ps[:, :, 0:A_PER_TILE]
-            )
-            nc.vector.tensor_tensor(
-                out=sums_view[:, :, NA : NA + NB],
-                in0=s_ps[:, :, A_PER_TILE:SUM_COLS],
-                in1=sums_view[:, :, NA : NA + NB],
-                op=ADD,
-            )
 
         for index in range(PASSES_1):
             regroup_piece(index)
@@ -321,22 +317,19 @@ def tile_bipartiteneuralmessagepassinglayer_pa_kernel(
                 quantise_hidden(rt, g, h_of[before])
 
         SUMS_BEHIND = 2
+        sums_ps = []
+        for half in range(OUT_HALVES):
+            half_ps = psum_plain.tile([P, BANK], F32, tag="plain")
+            sums_ps.append(half_ps)
         latent_of = {}
         for rt in range(ROW_TILES + SUMS_BEHIND):
             if rt < ROW_TILES:
                 latent_of[rt] = second_product(rt)
             if rt >= SUMS_BEHIND:
-                add_to_sums(rt - SUMS_BEHIND, latent_of[rt - SUMS_BEHIND])
+                add_to_sums(rt - SUMS_BEHIND, latent_of[rt - SUMS_BEHIND], sums_ps)
 
-        pairs = OUT_TILES // 2
-        back_ps = psum_plain.tile([P, pairs, P], F32, tag="plain")
-        for q in range(pairs):
-            nc.tensor.transpose(back_ps[:, q, :], sums_t[:, q * P : (q + 1) * P], ident[:])
-        back = keep.tile([P, pairs, P], F32)
-        nc.vector.tensor_copy(out=back[:], in_=back_ps[:])
-        sum_a_view = out_1.rearrange("i (q v f) -> v i q f", q=pairs, v=2)
-        sum_b_view = out_2.rearrange("j (q v f) -> v j q f", q=pairs, v=2)
-        for v in range(2):
-            first = v * (NA + NB)
-            nc.sync.dma_start(out=sum_a_view[v], in_=back[first : first + NA, :, :])
-            nc.sync.dma_start(out=sum_b_view[v], in_=back[first + NA : first + NA + NB, :, :])
+        sums = keep.tile([P, ED], F32)
+        nc.vector.tensor_copy(out=sums[:, 0:BANK], in_=sums_ps[0][:])
+        nc.scalar.copy(out=sums[:, BANK:ED], in_=sums_ps[1][:])
+        nc.sync.dma_start(out=out_1, in_=sums[0:NA, :])
+        nc.sync.dma_start(out=out_2, in_=sums[NA : NA + NB, :])

@@ -26,7 +26,7 @@ A_PER_TILE = P // NB
 PASSES_1 = K1 // K_PASS
 PASSES_2 = ED // K_PASS
 OUT_HALVES = ED // BANK
-OUT_TILES = ED // P
+E_TILES = ED // P
 
 FLOPS = 2 * ROWS * K1 * ED + 2 * ROWS * ED * ED
 
@@ -42,7 +42,7 @@ def tile_bipartiteneuralmessagepassinglayer_pa_kernel(
         keep = ctx.enter_context(tc.tile_pool(name="keep", bufs=1))
         grouped_w = ctx.enter_context(tc.tile_pool(name="grouped_w", bufs=2))
         grouped_x = ctx.enter_context(tc.tile_pool(name="grouped_x", bufs=2))
-        terms_pool = ctx.enter_context(tc.tile_pool(name="terms", bufs=3))
+        terms_pool = ctx.enter_context(tc.tile_pool(name="terms", bufs=4))
         hidden = ctx.enter_context(tc.tile_pool(name="hidden", bufs=3))
         latent_pool = ctx.enter_context(tc.tile_pool(name="latent", bufs=4))
         psum_x = ctx.enter_context(tc.psum_pool(name="psum_x", bufs=2))
@@ -96,17 +96,23 @@ def tile_bipartiteneuralmessagepassinglayer_pa_kernel(
         table_warmer = keep.tile([P, 1], F32)
         nc.scalar.activation(out=table_warmer[:], in_=ident[:, 0:1], func=RELU)
 
-        pick = keep.tile([P, NA, NB], BF16)
-        nc.vector.tensor_tensor(
-            out=pick[:],
-            in0=ident[:, 0:NA].unsqueeze(2).to_broadcast([P, NA, NB]),
-            in1=ident[:, NA : NA + NB].unsqueeze(1).to_broadcast([P, NA, NB]),
+        ident_bf = keep.tile([P, P], BF16)
+        masks.make_identity(nc, ident_bf[:])
+        nodes_ps = psum_plain.tile([P, E_TILES, P], BF16, tag="plain")
+        for e_tile in range(E_TILES):
+            nc.tensor.transpose(
+                nodes_ps[:, e_tile, :], node_rows[:, e_tile * P : (e_tile + 1) * P], ident_bf[:]
+            )
+        nodes_t = keep.tile([P, NA + NB + 1, E_TILES], F32)
+        nc.scalar.copy(
+            out=nodes_t[:], in_=nodes_ps[:, :, 0 : NA + NB + 1].rearrange("e t k -> e k t")
+        )
+        nc.gpsimd.tensor_tensor(
+            out=nodes_t[:, 0:NA, :],
+            in0=nodes_t[:, 0:NA, :],
+            in1=nodes_t[:, NA + NB : NA + NB + 1, :].to_broadcast([P, NA, E_TILES]),
             op=ADD,
         )
-        nc.vector.tensor_scalar_add(
-            out=pick[:], in0=pick[:], scalar1=ident[:, NA + NB : NA + NB + 1]
-        )
-        pick_cols = pick[:].rearrange("k i j -> k (i j)")
 
         of_a_node = keep.tile([P, A_PER_TILE], F32)
         nc.vector.tensor_reduce(
@@ -153,16 +159,17 @@ def tile_bipartiteneuralmessagepassinglayer_pa_kernel(
                 pieces.append((we2_raw[:, g, :, cols], we2_codes, we2_scales, g * ED + half * BANK))
         grouped_of = {}
 
-        def regroup_piece(index):
+        def regroup_piece(index, vector_cols):
             raw = pieces[index][0]
             grouped = grouped_w.tile([P, BANK * PACK], BF16, align_bytes=64)
             grouped_of[index] = grouped
             by_column = grouped[:].rearrange("p (n t) -> p n t", t=PACK)
-            first, second = slice(0, BANK // 2), slice(BANK // 2, BANK)
-            nc.vector.tensor_copy(
-                out=by_column[:, first, :].rearrange("p (n i) t -> p n t i", i=4),
-                in_=raw[:, :, first].rearrange("p t (n i) -> p n t i", i=4),
-            )
+            first, second = slice(0, vector_cols), slice(vector_cols, BANK)
+            if vector_cols > 0:
+                nc.vector.tensor_copy(
+                    out=by_column[:, first, :].rearrange("p (n i) t -> p n t i", i=4),
+                    in_=raw[:, :, first].rearrange("p t (n i) -> p n t i", i=4),
+                )
             nc.scalar.copy(
                 out=by_column[:, second, :].rearrange("p (n i) t -> p n t i", i=4),
                 in_=raw[:, :, second].rearrange("p t (n i) -> p n t i", i=4),
@@ -203,18 +210,17 @@ def tile_bipartiteneuralmessagepassinglayer_pa_kernel(
             )
 
         def node_terms(rt, g):
-            terms_ps = psum_plain.tile([P, PACK, P], F32, tag="plain")
-            for t in range(PACK):
-                e_tile = g * PACK + t
-                nc.tensor.matmul(
-                    terms_ps[:, t, :],
-                    lhsT=node_rows[:, e_tile * P : (e_tile + 1) * P],
-                    rhs=pick_cols[:, rt * P : (rt + 1) * P],
-                    start=True,
-                    stop=True,
-                )
-            terms = terms_pool.tile([P, P, PACK], F32)
-            nc.scalar.copy(out=terms[:], in_=terms_ps[:].rearrange("p t r -> p r t"))
+            shape = [P, A_PER_TILE, NB, PACK]
+            e_tiles = slice(g * PACK, (g + 1) * PACK)
+            terms = terms_pool.tile(shape, F32)
+            nc.gpsimd.tensor_tensor(
+                out=terms[:],
+                in0=nodes_t[:, rt * A_PER_TILE : (rt + 1) * A_PER_TILE, e_tiles]
+                .unsqueeze(2)
+                .to_broadcast(shape),
+                in1=nodes_t[:, NA : NA + NB, e_tiles].unsqueeze(1).to_broadcast(shape),
+                op=ADD,
+            )
             return terms
 
         def first_product(rt, g, terms):
@@ -235,7 +241,10 @@ def tile_bipartiteneuralmessagepassinglayer_pa_kernel(
                     )
             h_grouped = hidden.tile([P, P, PACK], BF16, align_bytes=64)
             nc.vector.tensor_tensor(
-                out=h_grouped[:], in0=h_ps[:].rearrange("p t r -> p r t"), in1=terms[:], op=ADD
+                out=h_grouped[:],
+                in0=h_ps[:].rearrange("p t r -> p r t"),
+                in1=terms[:].rearrange("p a j t -> p (a j) t"),
+                op=ADD,
             )
             return h_grouped
 
@@ -285,7 +294,7 @@ def tile_bipartiteneuralmessagepassinglayer_pa_kernel(
                 )
 
         for index in range(PASSES_1):
-            regroup_piece(index)
+            regroup_piece(index, BANK // 2)
             if index > 0:
                 quantise_piece(index - 1)
         quantise_piece(PASSES_1 - 1)
@@ -309,7 +318,7 @@ def tile_bipartiteneuralmessagepassinglayer_pa_kernel(
             if 0 <= unit < units:
                 index = PASSES_1 + unit // 2
                 if unit % 2 == 0:
-                    regroup_piece(index)
+                    regroup_piece(index, 0)
                 else:
                     quantise_piece(index)
             if before >= 0:

from contextlib import ExitStack

import concourse.masks as masks
import concourse.mybir as mybir

F32 = mybir.dt.float32
BF16 = mybir.dt.bfloat16
U32 = mybir.dt.uint32
U8 = mybir.dt.uint8
FP8X4 = mybir.dt.float8_e4m3fn_x4
ADD = mybir.AluOpType.add
RELU = mybir.ActivationFunctionType.Relu
AXIS_X = mybir.AxisListType.X

P = 128
PACK = 4
K_PASS = P * PACK
BANK = 512

NA, NB = 32, 32
ROWS = NA * NB
K1 = 2048
ED = 1024
ROW_TILES = ROWS // P
A_PER_TILE = P // NB
PASSES_1 = K1 // K_PASS
PASSES_2 = ED // K_PASS
OUT_HALVES = ED // BANK
E_TILES = ED // P

FLOPS = 2 * ROWS * K1 * ED + 2 * ROWS * ED * ED


def tile_bipartiteneuralmessagepassinglayer_pa_kernel(
    tc, edge_embeds, a_proj, b_proj, We, be1, We2, be2, out_0, out_1, out_2
):
    nc = tc.nc
    x_rows = edge_embeds.rearrange("a b k -> (a b) k")
    latent_rows = out_0.rearrange("a b f -> (a b) f")

    with ExitStack() as ctx:
        keep = ctx.enter_context(tc.tile_pool(name="keep", bufs=1))
        grouped_w = ctx.enter_context(tc.tile_pool(name="grouped_w", bufs=2))
        grouped_x = ctx.enter_context(tc.tile_pool(name="grouped_x", bufs=2))
        terms_pool = ctx.enter_context(tc.tile_pool(name="terms", bufs=4))
        hidden = ctx.enter_context(tc.tile_pool(name="hidden", bufs=3))
        latent_pool = ctx.enter_context(tc.tile_pool(name="latent", bufs=4))
        psum_x = ctx.enter_context(tc.psum_pool(name="psum_x", bufs=2))
        psum_plain = ctx.enter_context(tc.psum_pool(name="psum_plain", bufs=2))
        psum_mx = ctx.enter_context(tc.psum_pool(name="psum_mx", bufs=4))
        ctx.enter_context(tc.manual_schedule())

        node_rows = keep.tile([P, ED], BF16)
        nc.sync.dma_start(out=node_rows[0:NA, :], in_=a_proj)
        nc.sync.dma_start(out=node_rows[NA : NA + NB, :], in_=b_proj)
        nc.sync.dma_start(out=node_rows[NA + NB : P, :], in_=be1.partition_broadcast(P - NA - NB))

        we_raw = keep.tile([P, OUT_HALVES, PASSES_1, PACK, BANK], BF16)
        we2_raw = keep.tile([P, PASSES_2, PACK, ED], BF16)
        x_raw = keep.tile([P, ROW_TILES * K1], BF16)
        be2_all = keep.tile([P, ED], BF16)

        def load_we_piece(half, c):
            for u in range(2):
                first = c * K_PASS + u * (K_PASS // 2)
                nc.sync.dma_start(
                    out=we_raw[:, half, c, 2 * u : 2 * u + 2, :],
                    in_=We[
                        first : first + K_PASS // 2, half * BANK : (half + 1) * BANK
                    ].rearrange("(p e) n -> p e n", e=2),
                )

        def load_x(rt):
            nc.sync.dma_start(
                out=x_raw[:, rt * K1 : (rt + 1) * K1], in_=x_rows[rt * P : (rt + 1) * P, :]
            )

        for c in range(PASSES_1):
            load_we_piece(0, c)
        load_x(0)
        load_x(1)
        for c in range(PASSES_1):
            load_we_piece(1, c)
            load_x(2 + c)
        load_x(6)
        load_x(7)
        for g in range(PASSES_2):
            nc.sync.dma_start(
                out=we2_raw[:, g],
                in_=We2[g * K_PASS : (g + 1) * K_PASS, :].rearrange("(t p) n -> p t n", p=P),
            )
        nc.sync.dma_start(out=be2_all[:], in_=be2.partition_broadcast(P))

        ident = keep.tile([P, P], F32)
        masks.make_identity(nc, ident[:])
        table_warmer = keep.tile([P, 1], F32)
        nc.scalar.activation(out=table_warmer[:], in_=ident[:, 0:1], func=RELU)

        ident_bf = keep.tile([P, P], BF16)
        masks.make_identity(nc, ident_bf[:])
        nodes_ps = psum_plain.tile([P, E_TILES, P], BF16, tag="plain")
        for e_tile in range(E_TILES):
            nc.tensor.transpose(
                nodes_ps[:, e_tile, :], node_rows[:, e_tile * P : (e_tile + 1) * P], ident_bf[:]
            )
        nodes_t = keep.tile([P, NA + NB + 1, E_TILES], F32)
        nc.scalar.copy(
            out=nodes_t[:], in_=nodes_ps[:, :, 0 : NA + NB + 1].rearrange("e t k -> e k t")
        )
        nc.gpsimd.tensor_tensor(
            out=nodes_t[:, 0:NA, :],
            in0=nodes_t[:, 0:NA, :],
            in1=nodes_t[:, NA + NB : NA + NB + 1, :].to_broadcast([P, NA, E_TILES]),
            op=ADD,
        )

        of_a_node = keep.tile([P, A_PER_TILE], F32)
        nc.vector.tensor_reduce(
            out=of_a_node[:],
            in_=ident[:].rearrange("r (a j) -> r a j", a=A_PER_TILE),
            axis=AXIS_X,
            op=ADD,
        )
        of_b_node = keep.tile([P, NB], F32)
        nc.vector.tensor_reduce(
            out=of_b_node[:],
            in_=ident[:].rearrange("r (a j) -> r j a", a=A_PER_TILE),
            axis=AXIS_X,
            op=ADD,
        )
        summers = keep.tile([P, ROW_TILES, P], F32)
        nc.vector.memset(summers[:], 0.0)
        for rt in range(ROW_TILES):
            first_a = rt * A_PER_TILE
            nc.vector.tensor_copy(
                out=summers[:, rt, first_a : first_a + A_PER_TILE], in_=of_a_node[:]
            )
        nc.vector.tensor_copy(
            out=summers[:, :, NA : NA + NB],
            in_=of_b_node[:].unsqueeze(1).to_broadcast([P, ROW_TILES, NB]),
        )

        we_codes = keep.tile([P, PASSES_1 * ED], U32, align_bytes=64)
        we_scales = keep.tile([P, PASSES_1 * ED], U8, align_bytes=64)
        we2_codes = keep.tile([P, PASSES_2 * ED], U32, align_bytes=64)
        we2_scales = keep.tile([P, PASSES_2 * ED], U8, align_bytes=64)
        x_codes = keep.tile([P, ROW_TILES * PASSES_1 * P], U32, align_bytes=64)
        x_scales = keep.tile([P, ROW_TILES * PASSES_1 * P], U8, align_bytes=64)
        h_codes = keep.tile([P, ROW_TILES * PASSES_2 * P], U32, align_bytes=64)
        h_scales = keep.tile([P, ROW_TILES * PASSES_2 * P], U8, align_bytes=64)

        pieces = []
        for half in range(OUT_HALVES):
            for c in range(PASSES_1):
                pieces.append((we_raw[:, half, c], we_codes, we_scales, c * ED + half * BANK))
        for g in range(PASSES_2):
            for half in range(OUT_HALVES):
                cols = slice(half * BANK, (half + 1) * BANK)
                pieces.append((we2_raw[:, g, :, cols], we2_codes, we2_scales, g * ED + half * BANK))
        grouped_of = {}

        def regroup_piece(index, vector_cols):
            raw = pieces[index][0]
            grouped = grouped_w.tile([P, BANK * PACK], BF16, align_bytes=64)
            grouped_of[index] = grouped
            by_column = grouped[:].rearrange("p (n t) -> p n t", t=PACK)
            first, second = slice(0, vector_cols), slice(vector_cols, BANK)
            if vector_cols > 0:
                nc.vector.tensor_copy(
                    out=by_column[:, first, :].rearrange("p (n i) t -> p n t i", i=4),
                    in_=raw[:, :, first].rearrange("p t (n i) -> p n t i", i=4),
                )
            nc.scalar.copy(
                out=by_column[:, second, :].rearrange("p (n i) t -> p n t i", i=4),
                in_=raw[:, :, second].rearrange("p t (n i) -> p n t i", i=4),
            )

        def quantise_piece(index):
            codes, scales, first_col = pieces[index][1:]
            cols = slice(first_col, first_col + BANK)
            nc.vector.quantize_mx(
                out=codes[:, cols].bitcast(FP8X4),
                scales=scales[:, cols],
                in_=grouped_of[index][:],
            )

        x_words = x_raw[:].bitcast(F32)
        words_per_row = K1 // 2

        def transpose_x(rt):
            grouped = grouped_x.tile([P, PASSES_1 * P * PACK], BF16, align_bytes=64)
            grouped_words = grouped[:].bitcast(F32).rearrange(
                "p (c r u) -> p c r u", c=PASSES_1, u=2
            )
            for pair in range(PASSES_1 // 2):
                xt = psum_x.tile([P, 4, P], F32)
                for quarter in range(4):
                    first = rt * words_per_row + (pair * 4 + quarter) * P
                    nc.tensor.transpose(xt[:, quarter, :], x_words[:, first : first + P], ident[:])
                nc.scalar.copy(
                    out=grouped_words[:, 2 * pair : 2 * pair + 2, :, :],
                    in_=xt[:].rearrange("p (c u) r -> p c r u", u=2),
                )
            return grouped

        def quantise_x(rt, grouped):
            cols = slice(rt * PASSES_1 * P, (rt + 1) * PASSES_1 * P)
            nc.vector.quantize_mx(
                out=x_codes[:, cols].bitcast(FP8X4), scales=x_scales[:, cols], in_=grouped[:]
            )

        def node_terms(rt, g):
            shape = [P, A_PER_TILE, NB, PACK]
            e_tiles = slice(g * PACK, (g + 1) * PACK)
            terms = terms_pool.tile(shape, F32)
            nc.gpsimd.tensor_tensor(
                out=terms[:],
                in0=nodes_t[:, rt * A_PER_TILE : (rt + 1) * A_PER_TILE, e_tiles]
                .unsqueeze(2)
                .to_broadcast(shape),
                in1=nodes_t[:, NA : NA + NB, e_tiles].unsqueeze(1).to_broadcast(shape),
                op=ADD,
            )
            return terms

        def first_product(rt, g, terms):
            h_ps = psum_mx.tile([P, PACK, P], F32, tag="mx")
            for t in range(PACK):
                e_tile = g * PACK + t
                for c in range(PASSES_1):
                    w_cols = slice(c * ED + e_tile * P, c * ED + (e_tile + 1) * P)
                    r_cols = slice((rt * PASSES_1 + c) * P, (rt * PASSES_1 + c + 1) * P)
                    nc.tensor.matmul_mx(
                        out=h_ps[:, t, :],
                        lhsT=we_codes[:, w_cols].bitcast(FP8X4),
                        lhsT_scale=we_scales[:, w_cols],
                        rhs=x_codes[:, r_cols].bitcast(FP8X4),
                        rhs_scale=x_scales[:, r_cols],
                        start=(c == 0),
                        stop=(c == PASSES_1 - 1),
                    )
            h_grouped = hidden.tile([P, P, PACK], BF16, align_bytes=64)
            nc.vector.tensor_tensor(
                out=h_grouped[:],
                in0=h_ps[:].rearrange("p t r -> p r t"),
                in1=terms[:].rearrange("p a j t -> p (a j) t"),
                op=ADD,
            )
            return h_grouped

        def relu_hidden(h_grouped):
            nc.vector.tensor_scalar_max(out=h_grouped[:], in0=h_grouped[:], scalar1=0.0)

        def quantise_hidden(rt, g, h_grouped):
            cols = slice((rt * PASSES_2 + g) * P, (rt * PASSES_2 + g + 1) * P)
            nc.vector.quantize_mx(
                out=h_codes[:, cols].bitcast(FP8X4),
                scales=h_scales[:, cols],
                in_=h_grouped[:].rearrange("p r t -> p (r t)"),
            )

        def second_product(rt):
            latent = latent_pool.tile([P, ED], F32)
            for half in range(OUT_HALVES):
                o_ps = psum_mx.tile([P, BANK], F32, tag="mx")
                for g in range(PASSES_2):
                    r_cols = slice((rt * PASSES_2 + g) * P, (rt * PASSES_2 + g + 1) * P)
                    f_cols = slice(g * ED + half * BANK, g * ED + (half + 1) * BANK)
                    nc.tensor.matmul_mx(
                        out=o_ps[:],
                        lhsT=h_codes[:, r_cols].bitcast(FP8X4),
                        lhsT_scale=h_scales[:, r_cols],
                        rhs=we2_codes[:, f_cols].bitcast(FP8X4),
                        rhs_scale=we2_scales[:, f_cols],
                        start=(g == 0),
                        stop=(g == PASSES_2 - 1),
                    )
                cols = slice(half * BANK, (half + 1) * BANK)
                nc.vector.tensor_tensor(
                    out=latent[:, cols], in0=o_ps[:], in1=be2_all[:, cols], op=ADD
                )
                nc.scalar.activation(out=latent[:, cols], in_=latent[:, cols], func=RELU)
            nc.sync.dma_start(out=latent_rows[rt * P : (rt + 1) * P, :], in_=latent[:])
            return latent

        def add_to_sums(rt, latent, sums_ps):
            for half in range(OUT_HALVES):
                nc.tensor.matmul(
                    sums_ps[half][:],
                    lhsT=summers[:, rt, :],
                    rhs=latent[:, half * BANK : (half + 1) * BANK],
                    start=(rt == 0),
                    stop=(rt == ROW_TILES - 1),
                )

        for index in range(PASSES_1):
            regroup_piece(index, BANK // 2)
            if index > 0:
                quantise_piece(index - 1)
        quantise_piece(PASSES_1 - 1)

        units = PASSES_2 * ROW_TILES
        terms_of, h_of = {}, {}
        for unit in range(-1, units + 1):
            following, before = unit + 1, unit - 1
            if following < units:
                next_g, next_rt = divmod(following, ROW_TILES)
                if next_g == 0:
                    x_grouped = transpose_x(next_rt)
                    quantise_x(next_rt, x_grouped)
            if 0 <= unit < units:
                g, rt = divmod(unit, ROW_TILES)
                h_of[unit] = first_product(rt, g, terms_of[unit])
            if following < units:
                terms_of[following] = node_terms(next_rt, next_g)
            if before >= 0:
                relu_hidden(h_of[before])
            if 0 <= unit < units:
                index = PASSES_1 + unit // 2
                if unit % 2 == 0:
                    regroup_piece(index, 0)
                else:
                    quantise_piece(index)
            if before >= 0:
                g, rt = divmod(before, ROW_TILES)
                quantise_hidden(rt, g, h_of[before])

        SUMS_BEHIND = 2
        sums_ps = []
        for half in range(OUT_HALVES):
            half_ps = psum_plain.tile([P, BANK], F32, tag="plain")
            sums_ps.append(half_ps)
        latent_of = {}
        for rt in range(ROW_TILES + SUMS_BEHIND):
            if rt < ROW_TILES:
                latent_of[rt] = second_product(rt)
            if rt >= SUMS_BEHIND:
                add_to_sums(rt - SUMS_BEHIND, latent_of[rt - SUMS_BEHIND], sums_ps)

        sums = keep.tile([P, ED], F32)
        nc.vector.tensor_copy(out=sums[:, 0:BANK], in_=sums_ps[0][:])
        nc.scalar.copy(out=sums[:, BANK:ED], in_=sums_ps[1][:])
        nc.sync.dma_start(out=out_1, in_=sums[0:NA, :])
        nc.sync.dma_start(out=out_2, in_=sums[NA : NA + NB, :])
